import numpy as np
import ml_dtypes


def mxq(x, axis, fmt="e4m3"):
    dtype, down = {"e4m3": (ml_dtypes.float8_e4m3fn, 7), "e5m2": (ml_dtypes.float8_e5m2, 14)}[fmt]
    v = np.moveaxis(np.asarray(x, np.float32).astype(ml_dtypes.bfloat16).astype(np.float64), axis, -1)
    blocks = v.reshape(v.shape[:-1] + (-1, 32))
    amax = np.abs(blocks).max(-1, keepdims=True)
    byte = np.maximum(np.where(amax > 0, np.frexp(amax)[1] - 1 + 127, 0) - down, 1)
    scale = np.exp2(byte - 127.0)
    codes = (blocks / scale).astype(np.float32).astype(dtype).astype(np.float64)
    return np.moveaxis((codes * scale).reshape(v.shape), -1, axis)


WIDE = False


def mx_kscale(k):
    if not WIDE:
        return np.ones(k)
    levels = np.array([10, -10, 5, -5, 0])
    a = np.random.permutation(np.resize(levels, k // 512 * 4)).reshape(k // 512, 4)
    idx = np.arange(k)
    return np.exp2(a[idx // 512, idx % 128 // 32])


BF16 = ml_dtypes.bfloat16


def bf(x):
    return np.asarray(x, np.float32).astype(BF16)


def f64(x):
    return np.asarray(x).astype(np.float64)


E2M1 = np.array([0.0, 0.5, 1.0, 1.5, 2.0, 3.0, 4.0, 6.0, -0.0, -0.5, -1.0, -1.5, -2.0, -3.0, -4.0, -6.0])


def pack_weight(w, fmt):
    k, n = w.shape
    w = f64(bf(w)).reshape(k // 32, 32, n)
    amax = np.abs(w).max(1)
    if fmt == "e4m3":
        byte = np.frexp(amax)[1] - 1 + 127 - 7
    else:
        mant, ex = np.frexp(amax / 6.0)
        byte = np.where(mant > 0.5, ex, ex - 1) + 127
    byte = np.clip(np.where(amax > 0, byte, 1), 1, 254)
    scaled = (w * np.exp2(127.0 - byte)[:, None, :]).reshape(k, n).astype(np.float32)
    by_word = np.ascontiguousarray(scaled.reshape(k // 512, 128, 4, n).transpose(0, 1, 3, 2))
    if fmt == "e4m3":
        words = by_word.astype(ml_dtypes.float8_e4m3fn).view(np.uint8)
    else:
        c = by_word.astype(ml_dtypes.float4_e2m1fn).view(np.uint8) & 0xF
        words = c[..., 0::2] | (c[..., 1::2] << 4)
    return np.ascontiguousarray(words), np.ascontiguousarray(byte.astype(np.uint8).reshape(k // 512, 16, n))


def unpack_weight(words, scales, fmt):
    g, p, n, _ = words.shape
    if fmt == "e4m3":
        vals = np.ascontiguousarray(words).view(ml_dtypes.float8_e4m3fn).astype(np.float64)
    else:
        nib = np.empty((g, p, n, 4), np.uint8)
        nib[..., 0::2] = words & 0xF
        nib[..., 1::2] = words >> 4
        vals = E2M1[nib]
    vals = vals * np.repeat(np.exp2(scales.astype(np.float64) - 127.0), 8, axis=1)[..., None]
    return vals.transpose(0, 1, 3, 2).reshape(g * 512, n)


B, L, D, F = 4, 1024, 512, 512
FMT = "e4m3"


def silu(z):
    return z / (1.0 + np.exp(-z))


def sigmoid(z):
    return 1.0 / (1.0 + np.exp(-z))


def setup_inputs():
    s = mx_kscale(D)
    x = bf(np.random.standard_normal((B, L, D)) * s)
    W1_words, W1_scales = pack_weight(np.random.standard_normal((D, F)) / np.sqrt(D) / s[:, None], FMT)
    b1 = bf(np.random.standard_normal(F) * 0.3)
    W2g_words, W2g_scales = pack_weight(np.random.standard_normal((F, D)) * 2.4 / np.sqrt(F), FMT)
    b2g = bf(np.random.standard_normal(D) * 0.3)
    Wv_words, Wv_scales = pack_weight(np.random.standard_normal((D, D)) * 1.8 / np.sqrt(D) / s[:, None], FMT)
    bv = bf(np.random.standard_normal(D) * 0.3)
    return {
        "x": x,
        "W1_words": W1_words,
        "W1_scales": W1_scales,
        "b1": b1,
        "W2g_words": W2g_words,
        "W2g_scales": W2g_scales,
        "b2g": b2g,
        "Wv_words": Wv_words,
        "Wv_scales": Wv_scales,
        "bv": bv,
    }


def reference(x, W1_words, W1_scales, b1, W2g_words, W2g_scales, b2g, Wv_words, Wv_scales, bv):
    xq = mxq(f64(x), 2, "e4m3")
    h = silu((xq @ unpack_weight(W1_words, W1_scales, FMT)) + f64(b1))
    g = (mxq(h, 2, "e4m3") @ unpack_weight(W2g_words, W2g_scales, FMT)) + f64(b2g)
    return ((xq @ unpack_weight(Wv_words, Wv_scales, FMT)) + f64(bv)) * sigmoid(g)

@@ -1,0 +1,265 @@
+from contextlib import ExitStack
+
+import concourse.mybir as mybir
+from concourse.masks import make_identity
+
+F32 = mybir.dt.float32
+BF16 = mybir.dt.bfloat16
+I32 = mybir.dt.int32
+U32 = mybir.dt.uint32
+U8 = mybir.dt.uint8
+FP8X4 = mybir.dt.float8_e4m3fn_x4
+ACT = mybir.ActivationFunctionType
+ALU = mybir.AluOpType
+
+P = 128
+WIDTH = 512
+TOKENS = 4 * 1024
+TILES = 4
+GROUP = P * TILES
+GROUPS = TOKENS // GROUP
+CHUNKS = WIDTH // P
+BANK = 512
+
+FLOPS = 3 * 2 * TOKENS * WIDTH * WIDTH
+
+
+def tile_selectivemixing_pa_t_kernel(
+    tc, x, W1_words, W1_scales, b1, W2g_words, W2g_scales, b2g, Wv_words, Wv_scales, bv, out
+):
+    nc = tc.nc
+    x_groups = x.flatten_outer_dims().rearrange("(g p j) k -> g p j k", p=P, j=TILES)
+    out_groups = out.flatten_outer_dims().rearrange("(g p j) d -> g p j d", p=P, j=TILES)
+
+    with ExitStack() as ctx:
+        keep = ctx.enter_context(tc.tile_pool(name="keep", bufs=1))
+        grouped_pool = ctx.enter_context(tc.tile_pool(name="grouped", bufs=2))
+        work = ctx.enter_context(tc.tile_pool(name="work", bufs=3))
+        psum = ctx.enter_context(tc.psum_pool(name="psum", bufs=8))
+        ctx.enter_context(tc.manual_schedule())
+
+        def new_bank():
+            bank = psum.tile([P, BANK], F32, name="bank", tag="bank")
+            return bank
+
+        def weight_tiles(name):
+            codes = keep.tile([P, WIDTH], U32, name=name + "_codes", align_bytes=64)
+            plane = keep.tile([P, WIDTH], U8, name=name + "_plane", align_bytes=64)
+            nc.vector.memset(plane[:].bitcast(I32), 0)
+            return codes, plane
+
+        def load_weight(codes, plane, words, scales):
+            for r in range(4):
+                nc.sync.dma_start(
+                    out=plane[r:P:32, :].bitcast(I32), in_=scales[0, r:16:4, :].bitcast(I32)
+                )
+            nc.sync.dma_start(
+                out=codes[:].bitcast(I32),
+                in_=words[0].rearrange("p n t -> p (n t)").bitcast(I32),
+            )
+
+        def load_x(g):
+            x_sb = keep.tile([P, TILES, WIDTH], BF16, name="x%d" % g)
+            for half in range(2):
+                tiles = slice(2 * half, 2 * half + 2)
+                nc.sync.dma_start(out=x_sb[:, tiles, :], in_=x_groups[g][:, tiles, :])
+            return x_sb
+
+        w1_codes, w1_plane = weight_tiles("w1")
+        w2_codes, w2_plane = weight_tiles("w2")
+        wv_codes, wv_plane = weight_tiles("wv")
+        b1_row = keep.tile([P, WIDTH], BF16, name="b1_row")
+        nc.vector.memset(b1_row[:], 0.0)
+        bias_rows = keep.tile([P, P], BF16, name="bias_rows")
+        nc.vector.memset(bias_rows[:], 0.0)
+        ones = keep.tile([P, P], BF16, name="ones")
+        nc.vector.memset(ones[:], 1.0)
+        ident = keep.tile([P, P], F32, name="ident")
+        make_identity(nc, ident[:])
+
+        x_tiles = {}
+        x_tiles[0] = load_x(0)
+        load_weight(w1_codes, w1_plane, W1_words, W1_scales)
+        nc.sync.dma_start(out=b1_row[0:1, :], in_=b1.rearrange("(o f) -> o f", o=1))
+        nc.sync.dma_start(out=bias_rows[0:CHUNKS, :], in_=b2g.rearrange("(c m) -> c m", m=P))
+        nc.sync.dma_start(
+            out=bias_rows[CHUNKS : 2 * CHUNKS, :], in_=bv.rearrange("(c m) -> c m", m=P)
+        )
+        for g in range(1, GROUPS):
+            x_tiles[g] = load_x(g)
+        load_weight(w2_codes, w2_plane, W2g_words, W2g_scales)
+        load_weight(wv_codes, wv_plane, Wv_words, Wv_scales)
+
+        x_codes, x_planes, h_codes, h_planes = {}, {}, {}, {}
+        banks = {}
+        grouped = {}
+        h_tiles = {}
+
+        def transpose_words(kind, g, words_of):
+            for half in range(2):
+                bank = new_bank()
+                pieces = bank[:].rearrange("p (j u w) -> p j u w", j=2, u=2)
+                for j in range(2):
+                    for u in range(2):
+                        nc.tensor.transpose(
+                            out=pieces[:, j, u, :], in_=words_of(2 * half + j, u), identity=ident[:]
+                        )
+                banks[(kind, g, half)] = bank
+
+        def transpose_x(g):
+            words = x_tiles[g][:].bitcast(F32)
+            transpose_words("x", g, lambda j, u: words[:, j, u : WIDTH // 2 : 2])
+            x_grouped = grouped_pool.tile([P, 4 * GROUP], BF16, name="x_grouped", align_bytes=64)
+            grouped[("x", g)] = x_grouped
+
+        def transpose_h(g):
+            words = h_tiles[g][:].bitcast(F32)
+            transpose_words("h", g, lambda j, u: words[:, j, P * u : P * (u + 1)])
+            h_grouped = grouped_pool.tile([P, 4 * GROUP], BF16, name="h_grouped", align_bytes=64)
+            grouped[("h", g)] = h_grouped
+
+        def regroup(copy, kind, g, half):
+            words = grouped[(kind, g)][:].bitcast(F32).rearrange("p (j w u) -> p j w u", j=TILES, u=2)
+            copy(
+                out=words[:, 2 * half : 2 * half + 2, :, :],
+                in_=banks[(kind, g, half)][:].rearrange("p (j u w) -> p j w u", j=2, u=2),
+            )
+
+        def quantise(kind, g, codes_of, planes_of):
+            codes = keep.tile([P, GROUP], U32, name="%s_codes%d" % (kind, g), align_bytes=64)
+            plane = keep.tile([P, GROUP], U8, name="%s_plane%d" % (kind, g), align_bytes=64)
+            nc.vector.quantize_mx(out=codes[:].bitcast(FP8X4), scales=plane[:], in_=grouped[(kind, g)][:])
+            codes_of[g] = codes
+            planes_of[g] = plane
+
+        def first_layer(g):
+            for j in range(TILES):
+                cols = slice(P * j, P * (j + 1))
+                bank = new_bank()
+                nc.tensor.matmul_mx(
+                    out=bank[:],
+                    lhsT=x_codes[g][:, cols].bitcast(FP8X4),
+                    lhsT_scale=x_planes[g][:, cols],
+                    rhs=w1_codes[:].bitcast(FP8X4),
+                    rhs_scale=w1_plane[:],
+                    start=True,
+                    stop=True,
+                )
+                banks[("s1", g, j)] = bank
+            h_sb = work.tile([P, TILES, WIDTH], BF16, name="h_sb")
+            h_tiles[g] = h_sb
+
+        def by_piece(ap):
+            return ap.rearrange("p (q u e) -> p u q e", u=2, e=2)
+
+        def sorted_view(ap):
+            return ap.rearrange("p (u q e) -> p u q e", u=2, e=2)
+
+        def bias_and_silu(g, j):
+            z = work.tile([P, WIDTH], F32, name="z")
+            nc.vector.tensor_tensor(
+                out=sorted_view(z[:]), in0=by_piece(banks[("s1", g, j)][:]), in1=sorted_view(b1_all[:]), op=ALU.add
+            )
+            nc.scalar.activation(out=h_tiles[g][:, j, :], in_=z[:], func=ACT.Silu)
+
+        transpose_x(0)
+        regroup(nc.vector.tensor_copy, "x", 0, 0)
+        regroup(nc.scalar.copy, "x", 0, 1)
+        quantise("x", 0, x_codes, x_planes)
+        transpose_x(1)
+
+        b1_bank = new_bank()
+        nc.tensor.matmul(out=b1_bank[:], lhsT=ones[:], rhs=b1_row[:], start=True, stop=True)
+        b1_all = keep.tile([P, WIDTH], F32, name="b1_all")
+        nc.vector.tensor_copy(out=sorted_view(b1_all[:]), in_=by_piece(b1_bank[:]))
+        bias_rows_f32 = keep.tile([P, P], F32, name="bias_rows_f32")
+        nc.vector.tensor_copy(out=bias_rows_f32[:], in_=bias_rows[:])
+        bias_bank = new_bank()
+        nc.tensor.transpose(out=bias_bank[:, 0:P], in_=bias_rows_f32[:], identity=ident[:])
+        bias_cols = keep.tile([P, 2 * CHUNKS], F32, name="bias_cols")
+        nc.vector.tensor_copy(out=bias_cols[:], in_=bias_bank[:, 0 : 2 * CHUNKS])
+
+        for a in range(GROUPS + 1):
+            if a < GROUPS:
+                first_layer(a)
+            if a + 1 < GROUPS:
+                regroup(nc.scalar.copy, "x", a + 1, 1)
+            if a < GROUPS:
+                bias_and_silu(a, 0)
+            if a >= 1:
+                transpose_h(a - 1)
+                regroup(nc.scalar.copy, "h", a - 1, 0)
+                regroup(nc.scalar.copy, "h", a - 1, 1)
+            if a < GROUPS:
+                for j in range(1, TILES):
+                    bias_and_silu(a, j)
+            if a + 2 < GROUPS:
+                transpose_x(a + 2)
+            if a + 1 < GROUPS:
+                regroup(nc.vector.tensor_copy, "x", a + 1, 0)
+                quantise("x", a + 1, x_codes, x_planes)
+            if a >= 1:
+                quantise("h", a - 1, h_codes, h_planes)
+
+        products = {}
+
+        def gate_and_values(g):
+            product = work.tile([P, CHUNKS, GROUP], F32, name="product")
+            for c in range(CHUNKS):
+                cols = slice(P * c, P * (c + 1))
+                gate_bank = new_bank()
+                nc.tensor.matmul_mx(
+                    out=gate_bank[:],
+                    lhsT=w2_codes[:, cols].bitcast(FP8X4),
+                    lhsT_scale=w2_plane[:, cols],
+                    rhs=h_codes[g][:].bitcast(FP8X4),
+                    rhs_scale=h_planes[g][:],
+                    start=True,
+                    stop=True,
+                )
+                value_bank = new_bank()
+                nc.tensor.matmul_mx(
+                    out=value_bank[:],
+                    lhsT=wv_codes[:, cols].bitcast(FP8X4),
+                    lhsT_scale=wv_plane[:, cols],
+                    rhs=x_codes[g][:].bitcast(FP8X4),
+                    rhs_scale=x_planes[g][:],
+                    start=True,
+                    stop=True,
+                )
+                gate = work.tile([P, GROUP], F32, name="gate")
+                nc.scalar.activation(
+                    out=gate[:], in_=gate_bank[:], func=ACT.Sigmoid, bias=bias_cols[:, c : c + 1], scale=1.0
+                )
+                nc.vector.scalar_tensor_tensor(
+                    out=product[:, c, :],
+                    in0=value_bank[:],
+                    scalar=bias_cols[:, CHUNKS + c : CHUNKS + c + 1],
+                    in1=gate[:],
+                    op0=ALU.add,
+                    op1=ALU.mult,
+                )
+            products[g] = product
+
+        def store_group(g):
+            for j in range(TILES):
+                bank = new_bank()
+                for c in range(CHUNKS):
+                    nc.tensor.transpose(
+                        out=bank[:, P * c : P * (c + 1)],
+                        in_=products[g][:, c, P * j : P * (j + 1)],
+                        identity=ident[:],
+                    )
+                banks[("out", g, j)] = bank
+            out_sb = work.tile([P, TILES, WIDTH], F32, name="out_sb")
+            for half in range(2):
+                nc.scalar.copy(out=out_sb[:, 2 * half, :], in_=banks[("out", g, 2 * half)][:])
+                nc.vector.tensor_copy(out=out_sb[:, 2 * half + 1, :], in_=banks[("out", g, 2 * half + 1)][:])
+                tiles = slice(2 * half, 2 * half + 2)
+                nc.sync.dma_start(out=out_groups[g][:, tiles, :], in_=out_sb[:, tiles, :])
+
+        for b in range(GROUPS + 1):
+            if b < GROUPS:
+                gate_and_values(b)
+            if b >= 1:
+                store_group(b - 1)

@@ -186,18 +186,19 @@ def tile_selectivemixing_pa_t_kernel(
                 regroup(nc.scalar.copy, "x", a + 1, 1)
             if a < GROUPS:
                 bias_and_silu(a, 0)
+                bias_and_silu(a, 1)
+            if a + 1 < GROUPS:
+                regroup(nc.vector.tensor_copy, "x", a + 1, 0)
+                quantise("x", a + 1, x_codes, x_planes)
             if a >= 1:
                 transpose_h(a - 1)
                 regroup(nc.scalar.copy, "h", a - 1, 0)
                 regroup(nc.scalar.copy, "h", a - 1, 1)
             if a < GROUPS:
-                for j in range(1, TILES):
-                    bias_and_silu(a, j)
+                bias_and_silu(a, 2)
+                bias_and_silu(a, 3)
             if a + 2 < GROUPS:
                 transpose_x(a + 2)
-            if a + 1 < GROUPS:
-                regroup(nc.vector.tensor_copy, "x", a + 1, 0)
-                quantise("x", a + 1, x_codes, x_planes)
             if a >= 1:
                 quantise("h", a - 1, h_codes, h_planes)
 

@@ -33,8 +33,7 @@ def tile_selectivemixing_pa_t_kernel(
 
     with ExitStack() as ctx:
         keep = ctx.enter_context(tc.tile_pool(name="keep", bufs=1))
-        grouped_pool = ctx.enter_context(tc.tile_pool(name="grouped", bufs=2))
-        work = ctx.enter_context(tc.tile_pool(name="work", bufs=3))
+        work = ctx.enter_context(tc.tile_pool(name="work", bufs=2))
         psum = ctx.enter_context(tc.psum_pool(name="psum", bufs=8))
         ctx.enter_context(tc.manual_schedule())
 
@@ -85,69 +84,60 @@ def tile_selectivemixing_pa_t_kernel(
         nc.sync.dma_start(
             out=bias_rows[CHUNKS : 2 * CHUNKS, :], in_=bv.rearrange("(c m) -> c m", m=P)
         )
-        for g in range(1, GROUPS):
-            x_tiles[g] = load_x(g)
+        x_tiles[1] = load_x(1)
+        x_tiles[2] = load_x(2)
         load_weight(w2_codes, w2_plane, W2g_words, W2g_scales)
         load_weight(wv_codes, wv_plane, Wv_words, Wv_scales)
+        for g in range(3, GROUPS):
+            x_tiles[g] = load_x(g)
 
-        x_codes, x_planes, h_codes, h_planes = {}, {}, {}, {}
-        banks = {}
-        grouped = {}
-        h_tiles = {}
+        grouped, codes_of, planes_of = {}, {}, {}
+        sums, h_tiles, gates, products, out_tiles = {}, {}, {}, {}, {}
 
-        def transpose_words(kind, g, words_of):
-            for half in range(2):
-                bank = new_bank()
-                pieces = bank[:].rearrange("p (j u w) -> p j u w", j=2, u=2)
-                for j in range(2):
-                    for u in range(2):
-                        nc.tensor.transpose(
-                            out=pieces[:, j, u, :], in_=words_of(2 * half + j, u), identity=ident[:]
-                        )
-                banks[(kind, g, half)] = bank
-
-        def transpose_x(g):
-            words = x_tiles[g][:].bitcast(F32)
-            transpose_words("x", g, lambda j, u: words[:, j, u : WIDTH // 2 : 2])
-            x_grouped = grouped_pool.tile([P, 4 * GROUP], BF16, name="x_grouped", align_bytes=64)
-            grouped[("x", g)] = x_grouped
-
-        def transpose_h(g):
-            words = h_tiles[g][:].bitcast(F32)
-            transpose_words("h", g, lambda j, u: words[:, j, P * u : P * (u + 1)])
-            h_grouped = grouped_pool.tile([P, 4 * GROUP], BF16, name="h_grouped", align_bytes=64)
-            grouped[("h", g)] = h_grouped
-
-        def regroup(copy, kind, g, half):
+        def transpose_words(copy, kind, g, half, words_of):
+            if half == 0:
+                grouped_tile = work.tile([P, 4 * GROUP], BF16, name=kind + "_grouped", align_bytes=64)
+                grouped[(kind, g)] = grouped_tile
+            bank = new_bank()
+            pieces = bank[:].rearrange("p (j u w) -> p j u w", j=2, u=2)
+            for j in range(2):
+                for u in range(2):
+                    nc.tensor.transpose(
+                        out=pieces[:, j, u, :], in_=words_of(2 * half + j, u), identity=ident[:]
+                    )
             words = grouped[(kind, g)][:].bitcast(F32).rearrange("p (j w u) -> p j w u", j=TILES, u=2)
             copy(
                 out=words[:, 2 * half : 2 * half + 2, :, :],
-                in_=banks[(kind, g, half)][:].rearrange("p (j u w) -> p j w u", j=2, u=2),
+                in_=bank[:].rearrange("p (j u w) -> p j w u", j=2, u=2),
             )
 
-        def quantise(kind, g, codes_of, planes_of):
+        def transpose_x(copy, g, half):
+            words = x_tiles[g][:].bitcast(F32)
+            transpose_words(copy, "x", g, half, lambda j, u: words[:, j, u : WIDTH // 2 : 2])
+
+        def transpose_h(copy, g, half):
+            words = h_tiles[g][:].bitcast(F32)
+            transpose_words(copy, "h", g, half, lambda j, u: words[:, j, P * u : P * (u + 1)])
+
+        def quantise(kind, g):
             codes = keep.tile([P, GROUP], U32, name="%s_codes%d" % (kind, g), align_bytes=64)
             plane = keep.tile([P, GROUP], U8, name="%s_plane%d" % (kind, g), align_bytes=64)
             nc.vector.quantize_mx(out=codes[:].bitcast(FP8X4), scales=plane[:], in_=grouped[(kind, g)][:])
-            codes_of[g] = codes
-            planes_of[g] = plane
+            codes_of[(kind, g)] = codes
+            planes_of[(kind, g)] = plane
 
-        def first_layer(g):
-            for j in range(TILES):
-                cols = slice(P * j, P * (j + 1))
-                bank = new_bank()
-                nc.tensor.matmul_mx(
-                    out=bank[:],
-                    lhsT=x_codes[g][:, cols].bitcast(FP8X4),
-                    lhsT_scale=x_planes[g][:, cols],
-                    rhs=w1_codes[:].bitcast(FP8X4),
-                    rhs_scale=w1_plane[:],
-                    start=True,
-                    stop=True,
-                )
-                banks[("s1", g, j)] = bank
-            h_sb = work.tile([P, TILES, WIDTH], BF16, name="h_sb")
-            h_tiles[g] = h_sb
+        def mx_pass(lhs_codes, lhs_plane, rhs_codes, rhs_plane):
+            bank = new_bank()
+            nc.tensor.matmul_mx(
+                out=bank[:],
+                lhsT=lhs_codes.bitcast(FP8X4),
+                lhsT_scale=lhs_plane,
+                rhs=rhs_codes.bitcast(FP8X4),
+                rhs_scale=rhs_plane,
+                start=True,
+                stop=True,
+            )
+            return bank
 
         def by_piece(ap):
             return ap.rearrange("p (q u e) -> p u q e", u=2, e=2)
@@ -155,19 +145,79 @@ def tile_selectivemixing_pa_t_kernel(
         def sorted_view(ap):
             return ap.rearrange("p (u q e) -> p u q e", u=2, e=2)
 
-        def bias_and_silu(g, j):
-            z = work.tile([P, WIDTH], F32, name="z")
-            nc.vector.tensor_tensor(
-                out=sorted_view(z[:]), in0=by_piece(banks[("s1", g, j)][:]), in1=sorted_view(b1_all[:]), op=ALU.add
+        def first_layer(g, j):
+            if j == 0:
+                sum_tile = work.tile([P, TILES, WIDTH], F32, name="sum_tile")
+                sums[g] = sum_tile
+            cols = slice(P * j, P * (j + 1))
+            bank = mx_pass(
+                codes_of[("x", g)][:, cols], planes_of[("x", g)][:, cols], w1_codes[:], w1_plane[:]
             )
-            nc.scalar.activation(out=h_tiles[g][:, j, :], in_=z[:], func=ACT.Silu)
+            nc.vector.tensor_tensor(
+                out=sorted_view(sums[g][:, j, :]), in0=by_piece(bank[:]), in1=sorted_view(b1_all[:]), op=ALU.add
+            )
 
-        transpose_x(0)
-        regroup(nc.vector.tensor_copy, "x", 0, 0)
-        regroup(nc.scalar.copy, "x", 0, 1)
-        quantise("x", 0, x_codes, x_planes)
-        transpose_x(1)
+        def silu(g, j):
+            if j == 0:
+                h_sb = work.tile([P, TILES, WIDTH], BF16, name="h_sb")
+                h_tiles[g] = h_sb
+            nc.scalar.activation(out=h_tiles[g][:, j, :], in_=sums[g][:, j, :], func=ACT.Silu)
 
+        def gate(g, c):
+            if c == 0:
+                gate_tile = work.tile([P, CHUNKS, GROUP], F32, name="gate_tile")
+                gates[g] = gate_tile
+            cols = slice(P * c, P * (c + 1))
+            bank = mx_pass(
+                w2_codes[:, cols], w2_plane[:, cols], codes_of[("h", g)][:], planes_of[("h", g)][:]
+            )
+            nc.scalar.activation(
+                out=gates[g][:, c, :], in_=bank[:], func=ACT.Tanh, bias=half_b2g[:, c : c + 1], scale=0.5
+            )
+            nc.gpsimd.tensor_scalar(
+                out=gates[g][:, c, :], in0=gates[g][:, c, :], scalar1=0.5, scalar2=0.5, op0=ALU.mult, op1=ALU.add
+            )
+
+        def values(g, c):
+            if c == 0:
+                product = work.tile([P, CHUNKS, GROUP], F32, name="product")
+                products[g] = product
+            cols = slice(P * c, P * (c + 1))
+            bank = mx_pass(
+                wv_codes[:, cols], wv_plane[:, cols], codes_of[("x", g)][:], planes_of[("x", g)][:]
+            )
+            nc.vector.scalar_tensor_tensor(
+                out=products[g][:, c, :],
+                in0=bank[:],
+                scalar=bv_cols[:, c : c + 1],
+                in1=gates[g][:, c, :],
+                op0=ALU.add,
+                op1=ALU.mult,
+            )
+
+        def token_rows(copy, g, j):
+            if j == 0:
+                out_sb = work.tile([P, TILES, WIDTH], F32, name="out_sb")
+                out_tiles[g] = out_sb
+            bank = new_bank()
+            for c in range(CHUNKS):
+                nc.tensor.transpose(
+                    out=bank[:, P * c : P * (c + 1)],
+                    in_=products[g][:, c, P * j : P * (j + 1)],
+                    identity=ident[:],
+                )
+            copy(out=out_tiles[g][:, j, :], in_=bank[:])
+
+        def store(g, half):
+            tiles = slice(2 * half, 2 * half + 2)
+            nc.sync.dma_start(out=out_groups[g][:, tiles, :], in_=out_tiles[g][:, tiles, :])
+
+        def prepare_x(g):
+            transpose_x(nc.scalar.copy, g, 0)
+            transpose_x(nc.vector.tensor_copy, g, 1)
+            quantise("x", g)
+
+        prepare_x(0)
         b1_bank = new_bank()
         nc.tensor.matmul(out=b1_bank[:], lhsT=ones[:], rhs=b1_row[:], start=True, stop=True)
         b1_all = keep.tile([P, WIDTH], F32, name="b1_all")
@@ -176,91 +226,41 @@ def tile_selectivemixing_pa_t_kernel(
         nc.vector.tensor_copy(out=bias_rows_f32[:], in_=bias_rows[:])
         bias_bank = new_bank()
         nc.tensor.transpose(out=bias_bank[:, 0:P], in_=bias_rows_f32[:], identity=ident[:])
-        bias_cols = keep.tile([P, 2 * CHUNKS], F32, name="bias_cols")
-        nc.vector.tensor_copy(out=bias_cols[:], in_=bias_bank[:, 0 : 2 * CHUNKS])
+        half_b2g = keep.tile([P, CHUNKS], F32, name="half_b2g")
+        nc.vector.tensor_scalar_mul(out=half_b2g[:], in0=bias_bank[:, 0:CHUNKS], scalar1=0.5)
+        bv_cols = keep.tile([P, CHUNKS], F32, name="bv_cols")
+        nc.vector.tensor_copy(out=bv_cols[:], in_=bias_bank[:, CHUNKS : 2 * CHUNKS])
+        prepare_x(1)
 
-        for a in range(GROUPS + 1):
-            if a < GROUPS:
-                first_layer(a)
-            if a + 1 < GROUPS:
-                regroup(nc.scalar.copy, "x", a + 1, 1)
-            if a < GROUPS:
-                bias_and_silu(a, 0)
-                bias_and_silu(a, 1)
-            if a + 1 < GROUPS:
-                regroup(nc.vector.tensor_copy, "x", a + 1, 0)
-                quantise("x", a + 1, x_codes, x_planes)
-            if a >= 1:
-                transpose_h(a - 1)
-                regroup(nc.scalar.copy, "h", a - 1, 0)
-                regroup(nc.scalar.copy, "h", a - 1, 1)
-            if a < GROUPS:
-                bias_and_silu(a, 2)
-                bias_and_silu(a, 3)
-            if a + 2 < GROUPS:
-                transpose_x(a + 2)
-            if a >= 1:
-                quantise("h", a - 1, h_codes, h_planes)
+        def live(g):
+            return 0 <= g < GROUPS
 
-        products = {}
-
-        def gate_and_values(g):
-            product = work.tile([P, CHUNKS, GROUP], F32, name="product")
-            for c in range(CHUNKS):
-                cols = slice(P * c, P * (c + 1))
-                gate_bank = new_bank()
-                nc.tensor.matmul_mx(
-                    out=gate_bank[:],
-                    lhsT=w2_codes[:, cols].bitcast(FP8X4),
-                    lhsT_scale=w2_plane[:, cols],
-                    rhs=h_codes[g][:].bitcast(FP8X4),
-                    rhs_scale=h_planes[g][:],
-                    start=True,
-                    stop=True,
-                )
-                value_bank = new_bank()
-                nc.tensor.matmul_mx(
-                    out=value_bank[:],
-                    lhsT=wv_codes[:, cols].bitcast(FP8X4),
-                    lhsT_scale=wv_plane[:, cols],
-                    rhs=x_codes[g][:].bitcast(FP8X4),
-                    rhs_scale=x_planes[g][:],
-                    start=True,
-                    stop=True,
-                )
-                gate = work.tile([P, GROUP], F32, name="gate")
-                nc.scalar.activation(
-                    out=gate[:], in_=gate_bank[:], func=ACT.Sigmoid, bias=bias_cols[:, c : c + 1], scale=1.0
-                )
-                nc.vector.scalar_tensor_tensor(
-                    out=product[:, c, :],
-                    in0=value_bank[:],
-                    scalar=bias_cols[:, CHUNKS + c : CHUNKS + c + 1],
-                    in1=gate[:],
-                    op0=ALU.add,
-                    op1=ALU.mult,
-                )
-            products[g] = product
-
-        def store_group(g):
-            for j in range(TILES):
-                bank = new_bank()
+        for a in range(GROUPS + 3):
+            if live(a + 2):
+                transpose_x(nc.scalar.copy, a + 2, 0)
+            if live(a - 1):
+                transpose_h(nc.scalar.copy, a - 1, 0)
+            for i in range(4):
+                if live(a):
+                    first_layer(a, i)
+                if live(a - 2):
+                    gate(a - 2, i)
+            if live(a):
+                for j in range(TILES):
+                    silu(a, j)
+            if live(a - 1):
+                transpose_h(nc.vector.tensor_copy, a - 1, 1)
+                quantise("h", a - 1)
+            if live(a - 2):
                 for c in range(CHUNKS):
-                    nc.tensor.transpose(
-                        out=bank[:, P * c : P * (c + 1)],
-                        in_=products[g][:, c, P * j : P * (j + 1)],
-                        identity=ident[:],
-                    )
-                banks[("out", g, j)] = bank
-            out_sb = work.tile([P, TILES, WIDTH], F32, name="out_sb")
-            for half in range(2):
-                nc.scalar.copy(out=out_sb[:, 2 * half, :], in_=banks[("out", g, 2 * half)][:])
-                nc.vector.tensor_copy(out=out_sb[:, 2 * half + 1, :], in_=banks[("out", g, 2 * half + 1)][:])
-                tiles = slice(2 * half, 2 * half + 2)
-                nc.sync.dma_start(out=out_groups[g][:, tiles, :], in_=out_sb[:, tiles, :])
-
-        for b in range(GROUPS + 1):
-            if b < GROUPS:
-                gate_and_values(b)
-            if b >= 1:
-                store_group(b - 1)
+                    values(a - 2, c)
+            if live(a + 2):
+                transpose_x(nc.vector.tensor_copy, a + 2, 1)
+                quantise("x", a + 2)
+            if live(a - 3):
+                token_rows(nc.scalar.copy, a - 3, 0)
+                token_rows(nc.scalar.copy, a - 3, 1)
+                store(a - 3, 0)
+                token_rows(nc.vector.tensor_copy, a - 3, 2)
+                token_rows(nc.scalar.copy, a - 3, 3)
+                store(a - 3, 1)

@@ -238,6 +238,7 @@ def tile_selectivemixing_pa_t_kernel(
         for a in range(GROUPS + 3):
             if live(a + 2):
                 transpose_x(nc.scalar.copy, a + 2, 0)
+                transpose_x(nc.scalar.copy, a + 2, 1)
             if live(a - 1):
                 transpose_h(nc.scalar.copy, a - 1, 0)
             for i in range(4):
@@ -255,7 +256,6 @@ def tile_selectivemixing_pa_t_kernel(
                 for c in range(CHUNKS):
                     values(a - 2, c)
             if live(a + 2):
-                transpose_x(nc.vector.tensor_copy, a + 2, 1)
                 quantise("x", a + 2)
             if live(a - 3):
                 token_rows(nc.scalar.copy, a - 3, 0)

@@ -13,6 +13,7 @@ ACT = mybir.ActivationFunctionType
 ALU = mybir.AluOpType
 
 P = 128
+PACK = 4
 WIDTH = 512
 TOKENS = 4 * 1024
 TILES = 4
@@ -44,14 +45,16 @@ def tile_selectivemixing_pa_t_kernel(
         def weight_tiles(name):
             codes = keep.tile([P, WIDTH], U32, name=name + "_codes", align_bytes=64)
             plane = keep.tile([P, WIDTH], U8, name=name + "_plane", align_bytes=64)
-            nc.vector.memset(plane[:].bitcast(I32), 0)
             return codes, plane
 
-        def load_weight(codes, plane, words, scales):
+        def load_scales(plane, scales):
+            nc.vector.memset(plane[:].bitcast(I32), 0)
             for r in range(4):
                 nc.sync.dma_start(
                     out=plane[r:P:32, :].bitcast(I32), in_=scales[0, r:16:4, :].bitcast(I32)
                 )
+
+        def load_codes(codes, words):
             nc.sync.dma_start(
                 out=codes[:].bitcast(I32),
                 in_=words[0].rearrange("p n t -> p (n t)").bitcast(I32),
@@ -64,60 +67,67 @@ def tile_selectivemixing_pa_t_kernel(
                 nc.sync.dma_start(out=x_sb[:, tiles, :], in_=x_groups[g][:, tiles, :])
             return x_sb
 
+        w1_given_codes, w1_given_plane = weight_tiles("w1_given")
         w1_codes, w1_plane = weight_tiles("w1")
         w2_codes, w2_plane = weight_tiles("w2")
         wv_codes, wv_plane = weight_tiles("wv")
-        b1_row = keep.tile([P, WIDTH], BF16, name="b1_row")
-        nc.vector.memset(b1_row[:], 0.0)
+        b1_bf16 = keep.tile([P, PACK], BF16, name="b1_bf16")
         bias_rows = keep.tile([P, P], BF16, name="bias_rows")
-        nc.vector.memset(bias_rows[:], 0.0)
-        ones = keep.tile([P, P], BF16, name="ones")
-        nc.vector.memset(ones[:], 1.0)
         ident = keep.tile([P, P], F32, name="ident")
         make_identity(nc, ident[:])
 
         x_tiles = {}
+        load_scales(w1_given_plane, W1_scales)
+        nc.sync.dma_start(out=b1_bf16[:], in_=b1.rearrange("(p t) -> p t", t=PACK))
+        load_codes(w1_given_codes, W1_words)
         x_tiles[0] = load_x(0)
-        load_weight(w1_codes, w1_plane, W1_words, W1_scales)
-        nc.sync.dma_start(out=b1_row[0:1, :], in_=b1.rearrange("(o f) -> o f", o=1))
+        nc.vector.memset(bias_rows[:], 0.0)
         nc.sync.dma_start(out=bias_rows[0:CHUNKS, :], in_=b2g.rearrange("(c m) -> c m", m=P))
         nc.sync.dma_start(
             out=bias_rows[CHUNKS : 2 * CHUNKS, :], in_=bv.rearrange("(c m) -> c m", m=P)
         )
         x_tiles[1] = load_x(1)
+        load_scales(w2_plane, W2g_scales)
+        load_codes(w2_codes, W2g_words)
         x_tiles[2] = load_x(2)
-        load_weight(w2_codes, w2_plane, W2g_words, W2g_scales)
-        load_weight(wv_codes, wv_plane, Wv_words, Wv_scales)
+        load_scales(wv_plane, Wv_scales)
+        load_codes(wv_codes, Wv_words)
         for g in range(3, GROUPS):
             x_tiles[g] = load_x(g)
 
-        grouped, codes_of, planes_of = {}, {}, {}
-        sums, h_tiles, gates, products, out_tiles = {}, {}, {}, {}, {}
+        nc.vector.tensor_copy(
+            out=w1_codes[:].bitcast(I32).rearrange("p (t m) -> p t m", t=PACK),
+            in_=w1_given_codes[:].bitcast(I32).rearrange("p (m t) -> p t m", t=PACK),
+        )
+        nc.vector.tensor_copy(
+            out=w1_plane[:].rearrange("p (t m) -> p m t", t=PACK),
+            in_=w1_given_plane[:].rearrange("p (m t) -> p m t", t=PACK),
+        )
+        b1_cols = keep.tile([P, PACK], F32, name="b1_cols")
+        nc.vector.tensor_copy(out=b1_cols[:], in_=b1_bf16[:])
 
-        def transpose_words(copy, kind, g, half, words_of):
+        grouped, codes_of, planes_of = {}, {}, {}
+        h_tiles, gates, products, out_tiles = {}, {}, {}, {}
+
+        def transpose_x(copy, g, half):
             if half == 0:
-                grouped_tile = work.tile([P, 4 * GROUP], BF16, name=kind + "_grouped", align_bytes=64)
-                grouped[(kind, g)] = grouped_tile
+                x_grouped = work.tile([P, PACK * GROUP], BF16, name="x_grouped", align_bytes=64)
+                grouped[("x", g)] = x_grouped
+            given = x_tiles[g][:].bitcast(F32)
             bank = new_bank()
             pieces = bank[:].rearrange("p (j u w) -> p j u w", j=2, u=2)
             for j in range(2):
                 for u in range(2):
                     nc.tensor.transpose(
-                        out=pieces[:, j, u, :], in_=words_of(2 * half + j, u), identity=ident[:]
+                        out=pieces[:, j, u, :],
+                        in_=given[:, 2 * half + j, u : WIDTH // 2 : 2],
+                        identity=ident[:],
                     )
-            words = grouped[(kind, g)][:].bitcast(F32).rearrange("p (j w u) -> p j w u", j=TILES, u=2)
+            words = grouped[("x", g)][:].bitcast(F32).rearrange("p (j w u) -> p j w u", j=TILES, u=2)
             copy(
                 out=words[:, 2 * half : 2 * half + 2, :, :],
                 in_=bank[:].rearrange("p (j u w) -> p j w u", j=2, u=2),
             )
-
-        def transpose_x(copy, g, half):
-            words = x_tiles[g][:].bitcast(F32)
-            transpose_words(copy, "x", g, half, lambda j, u: words[:, j, u : WIDTH // 2 : 2])
-
-        def transpose_h(copy, g, half):
-            words = h_tiles[g][:].bitcast(F32)
-            transpose_words(copy, "h", g, half, lambda j, u: words[:, j, P * u : P * (u + 1)])
 
         def quantise(kind, g):
             codes = keep.tile([P, GROUP], U32, name="%s_codes%d" % (kind, g), align_bytes=64)
@@ -126,51 +136,42 @@ def tile_selectivemixing_pa_t_kernel(
             codes_of[(kind, g)] = codes
             planes_of[(kind, g)] = plane
 
-        def mx_pass(lhs_codes, lhs_plane, rhs_codes, rhs_plane):
+        def mx_pass(weight_codes, weight_plane, chunk, kind, g):
+            cols = slice(P * chunk, P * (chunk + 1))
             bank = new_bank()
             nc.tensor.matmul_mx(
                 out=bank[:],
-                lhsT=lhs_codes.bitcast(FP8X4),
-                lhsT_scale=lhs_plane,
-                rhs=rhs_codes.bitcast(FP8X4),
-                rhs_scale=rhs_plane,
+                lhsT=weight_codes[:, cols].bitcast(FP8X4),
+                lhsT_scale=weight_plane[:, cols],
+                rhs=codes_of[(kind, g)][:].bitcast(FP8X4),
+                rhs_scale=planes_of[(kind, g)][:],
                 start=True,
                 stop=True,
             )
             return bank
 
-        def by_piece(ap):
-            return ap.rearrange("p (q u e) -> p u q e", u=2, e=2)
-
-        def sorted_view(ap):
-            return ap.rearrange("p (u q e) -> p u q e", u=2, e=2)
-
-        def first_layer(g, j):
-            if j == 0:
-                sum_tile = work.tile([P, TILES, WIDTH], F32, name="sum_tile")
-                sums[g] = sum_tile
-            cols = slice(P * j, P * (j + 1))
-            bank = mx_pass(
-                codes_of[("x", g)][:, cols], planes_of[("x", g)][:, cols], w1_codes[:], w1_plane[:]
-            )
-            nc.vector.tensor_tensor(
-                out=sorted_view(sums[g][:, j, :]), in0=by_piece(bank[:]), in1=sorted_view(b1_all[:]), op=ALU.add
+        def first_layer(g, t):
+            if t == 0:
+                h_rows = work.tile([P, PACK, GROUP], BF16, name="h_rows")
+                h_tiles[g] = h_rows
+            bank = mx_pass(w1_codes, w1_plane, t, "x", g)
+            nc.scalar.activation(
+                out=h_tiles[g][:, t, :], in_=bank[:], func=ACT.Silu, bias=b1_cols[:, t : t + 1]
             )
 
-        def silu(g, j):
-            if j == 0:
-                h_sb = work.tile([P, TILES, WIDTH], BF16, name="h_sb")
-                h_tiles[g] = h_sb
-            nc.scalar.activation(out=h_tiles[g][:, j, :], in_=sums[g][:, j, :], func=ACT.Silu)
+        def interleave_h(g):
+            h_grouped = work.tile([P, PACK * GROUP], BF16, name="h_grouped", align_bytes=64)
+            grouped[("h", g)] = h_grouped
+            nc.vector.tensor_copy(
+                out=h_grouped[:].rearrange("p (c t) -> p c t", t=PACK),
+                in_=h_tiles[g][:].rearrange("p t c -> p c t"),
+            )
 
         def gate(g, c):
             if c == 0:
                 gate_tile = work.tile([P, CHUNKS, GROUP], F32, name="gate_tile")
                 gates[g] = gate_tile
-            cols = slice(P * c, P * (c + 1))
-            bank = mx_pass(
-                w2_codes[:, cols], w2_plane[:, cols], codes_of[("h", g)][:], planes_of[("h", g)][:]
-            )
+            bank = mx_pass(w2_codes, w2_plane, c, "h", g)
             nc.scalar.activation(
                 out=gates[g][:, c, :], in_=bank[:], func=ACT.Tanh, bias=half_b2g[:, c : c + 1], scale=0.5
             )
@@ -182,10 +183,7 @@ def tile_selectivemixing_pa_t_kernel(
             if c == 0:
                 product = work.tile([P, CHUNKS, GROUP], F32, name="product")
                 products[g] = product
-            cols = slice(P * c, P * (c + 1))
-            bank = mx_pass(
-                wv_codes[:, cols], wv_plane[:, cols], codes_of[("x", g)][:], planes_of[("x", g)][:]
-            )
+            bank = mx_pass(wv_codes, wv_plane, c, "x", g)
             nc.vector.scalar_tensor_tensor(
                 out=products[g][:, c, :],
                 in0=bank[:],
@@ -212,16 +210,47 @@ def tile_selectivemixing_pa_t_kernel(
             tiles = slice(2 * half, 2 * half + 2)
             nc.sync.dma_start(out=out_groups[g][:, tiles, :], in_=out_tiles[g][:, tiles, :])
 
-        def prepare_x(g):
-            transpose_x(nc.scalar.copy, g, 0)
-            transpose_x(nc.vector.tensor_copy, g, 1)
-            quantise("x", g)
+        def live(g):
+            return 0 <= g < GROUPS
 
-        prepare_x(0)
-        b1_bank = new_bank()
-        nc.tensor.matmul(out=b1_bank[:], lhsT=ones[:], rhs=b1_row[:], start=True, stop=True)
-        b1_all = keep.tile([P, WIDTH], F32, name="b1_all")
-        nc.vector.tensor_copy(out=sorted_view(b1_all[:]), in_=by_piece(b1_bank[:]))
+        def one_round(a):
+            load = {"scalar": 4 * live(a) + 4 * live(a - 2), "vector": 4 * live(a - 3) + 3 * live(a - 1) + live(a + 2)}
+
+            def copier():
+                if load["scalar"] <= load["vector"]:
+                    load["scalar"] += 1
+                    return nc.scalar.copy
+                load["vector"] += 1
+                return nc.vector.tensor_copy
+
+            if live(a - 1):
+                interleave_h(a - 1)
+            for i in range(4):
+                if live(a - 3):
+                    values(a - 3, i)
+                if live(a - 2):
+                    gate(a - 2, i)
+                if i == 0 and live(a - 1):
+                    quantise("h", a - 1)
+            if live(a):
+                for t in range(PACK):
+                    first_layer(a, t)
+            if live(a + 2):
+                transpose_x(copier(), a + 2, 0)
+                transpose_x(copier(), a + 2, 1)
+            if live(a - 4):
+                token_rows(copier(), a - 4, 0)
+                token_rows(copier(), a - 4, 1)
+                store(a - 4, 0)
+            if live(a + 2):
+                quantise("x", a + 2)
+            if live(a - 4):
+                token_rows(copier(), a - 4, 2)
+                token_rows(copier(), a - 4, 3)
+                store(a - 4, 1)
+
+        one_round(-2)
+        one_round(-1)
         bias_rows_f32 = keep.tile([P, P], F32, name="bias_rows_f32")
         nc.vector.tensor_copy(out=bias_rows_f32[:], in_=bias_rows[:])
         bias_bank = new_bank()
@@ -230,37 +259,5 @@ def tile_selectivemixing_pa_t_kernel(
         nc.vector.tensor_scalar_mul(out=half_b2g[:], in0=bias_bank[:, 0:CHUNKS], scalar1=0.5)
         bv_cols = keep.tile([P, CHUNKS], F32, name="bv_cols")
         nc.vector.tensor_copy(out=bv_cols[:], in_=bias_bank[:, CHUNKS : 2 * CHUNKS])
-        prepare_x(1)
-
-        def live(g):
-            return 0 <= g < GROUPS
-
-        for a in range(GROUPS + 3):
-            if live(a + 2):
-                transpose_x(nc.scalar.copy, a + 2, 0)
-                transpose_x(nc.scalar.copy, a + 2, 1)
-            if live(a - 1):
-                transpose_h(nc.scalar.copy, a - 1, 0)
-            for i in range(4):
-                if live(a):
-                    first_layer(a, i)
-                if live(a - 2):
-                    gate(a - 2, i)
-            if live(a):
-                for j in range(TILES):
-                    silu(a, j)
-            if live(a - 1):
-                transpose_h(nc.vector.tensor_copy, a - 1, 1)
-                quantise("h", a - 1)
-            if live(a - 2):
-                for c in range(CHUNKS):
-                    values(a - 2, c)
-            if live(a + 2):
-                quantise("x", a + 2)
-            if live(a - 3):
-                token_rows(nc.scalar.copy, a - 3, 0)
-                token_rows(nc.scalar.copy, a - 3, 1)
-                store(a - 3, 0)
-                token_rows(nc.vector.tensor_copy, a - 3, 2)
-                token_rows(nc.scalar.copy, a - 3, 3)
-                store(a - 3, 1)
+        for a in range(0, GROUPS + 4):
+            one_round(a)

@@ -78,9 +78,9 @@ def tile_selectivemixing_pa_t_kernel(
 
         x_tiles = {}
         load_scales(w1_given_plane, W1_scales)
-        nc.sync.dma_start(out=b1_bf16[:], in_=b1.rearrange("(p t) -> p t", t=PACK))
-        load_codes(w1_given_codes, W1_words)
         x_tiles[0] = load_x(0)
+        load_codes(w1_given_codes, W1_words)
+        nc.sync.dma_start(out=b1_bf16[:], in_=b1.rearrange("(p t) -> p t", t=PACK))
         nc.vector.memset(bias_rows[:], 0.0)
         nc.sync.dma_start(out=bias_rows[0:CHUNKS, :], in_=b2g.rearrange("(c m) -> c m", m=P))
         nc.sync.dma_start(
@@ -96,12 +96,12 @@ def tile_selectivemixing_pa_t_kernel(
             x_tiles[g] = load_x(g)
 
         nc.vector.tensor_copy(
-            out=w1_codes[:].bitcast(I32).rearrange("p (t m) -> p t m", t=PACK),
-            in_=w1_given_codes[:].bitcast(I32).rearrange("p (m t) -> p t m", t=PACK),
-        )
-        nc.vector.tensor_copy(
             out=w1_plane[:].rearrange("p (t m) -> p m t", t=PACK),
             in_=w1_given_plane[:].rearrange("p (m t) -> p m t", t=PACK),
+        )
+        nc.vector.tensor_copy(
+            out=w1_codes[:].bitcast(I32).rearrange("p (t m) -> p t m", t=PACK),
+            in_=w1_given_codes[:].bitcast(I32).rearrange("p (m t) -> p t m", t=PACK),
         )
         b1_cols = keep.tile([P, PACK], F32, name="b1_cols")
         nc.vector.tensor_copy(out=b1_cols[:], in_=b1_bf16[:])
@@ -225,26 +225,25 @@ def tile_selectivemixing_pa_t_kernel(
 
             if live(a - 1):
                 interleave_h(a - 1)
-            for i in range(4):
-                if live(a - 3):
-                    values(a - 3, i)
-                if live(a - 2):
-                    gate(a - 2, i)
-                if i == 0 and live(a - 1):
-                    quantise("h", a - 1)
             if live(a):
                 for t in range(PACK):
                     first_layer(a, t)
             if live(a + 2):
                 transpose_x(copier(), a + 2, 0)
                 transpose_x(copier(), a + 2, 1)
+            if live(a - 1):
+                quantise("h", a - 1)
+            for i in range(4):
+                if live(a - 3):
+                    values(a - 3, i)
+                if live(a - 2):
+                    gate(a - 2, i)
+                if i == 0 and live(a + 2):
+                    quantise("x", a + 2)
             if live(a - 4):
                 token_rows(copier(), a - 4, 0)
                 token_rows(copier(), a - 4, 1)
                 store(a - 4, 0)
-            if live(a + 2):
-                quantise("x", a + 2)
-            if live(a - 4):
                 token_rows(copier(), a - 4, 2)
                 token_rows(copier(), a - 4, 3)
                 store(a - 4, 1)
@@ -253,11 +252,12 @@ def tile_selectivemixing_pa_t_kernel(
         one_round(-1)
         bias_rows_f32 = keep.tile([P, P], F32, name="bias_rows_f32")
         nc.vector.tensor_copy(out=bias_rows_f32[:], in_=bias_rows[:])
+        one_round(0)
         bias_bank = new_bank()
         nc.tensor.transpose(out=bias_bank[:, 0:P], in_=bias_rows_f32[:], identity=ident[:])
         half_b2g = keep.tile([P, CHUNKS], F32, name="half_b2g")
         nc.vector.tensor_scalar_mul(out=half_b2g[:], in0=bias_bank[:, 0:CHUNKS], scalar1=0.5)
         bv_cols = keep.tile([P, CHUNKS], F32, name="bv_cols")
         nc.vector.tensor_copy(out=bv_cols[:], in_=bias_bank[:, CHUNKS : 2 * CHUNKS])
-        for a in range(0, GROUPS + 4):
+        for a in range(1, GROUPS + 4):
             one_round(a)

@@ -35,6 +35,7 @@ def tile_selectivemixing_pa_t_kernel(
     with ExitStack() as ctx:
         keep = ctx.enter_context(tc.tile_pool(name="keep", bufs=1))
         work = ctx.enter_context(tc.tile_pool(name="work", bufs=2))
+        held = ctx.enter_context(tc.tile_pool(name="held", bufs=4))
         psum = ctx.enter_context(tc.psum_pool(name="psum", bufs=8))
         ctx.enter_context(tc.manual_schedule())
 
@@ -72,7 +73,9 @@ def tile_selectivemixing_pa_t_kernel(
         w2_codes, w2_plane = weight_tiles("w2")
         wv_codes, wv_plane = weight_tiles("wv")
         b1_bf16 = keep.tile([P, PACK], BF16, name="b1_bf16")
-        bias_rows = keep.tile([P, P], BF16, name="bias_rows")
+        b2g_rows = keep.tile([P, P], BF16, name="b2g_rows")
+        bv_row = keep.tile([P, WIDTH], BF16, name="bv_row")
+        ones = keep.tile([P, P], BF16, name="ones")
         ident = keep.tile([P, P], F32, name="ident")
         make_identity(nc, ident[:])
 
@@ -81,17 +84,17 @@ def tile_selectivemixing_pa_t_kernel(
         x_tiles[0] = load_x(0)
         load_codes(w1_given_codes, W1_words)
         nc.sync.dma_start(out=b1_bf16[:], in_=b1.rearrange("(p t) -> p t", t=PACK))
-        nc.vector.memset(bias_rows[:], 0.0)
-        nc.sync.dma_start(out=bias_rows[0:CHUNKS, :], in_=b2g.rearrange("(c m) -> c m", m=P))
-        nc.sync.dma_start(
-            out=bias_rows[CHUNKS : 2 * CHUNKS, :], in_=bv.rearrange("(c m) -> c m", m=P)
-        )
         x_tiles[1] = load_x(1)
-        load_scales(w2_plane, W2g_scales)
-        load_codes(w2_codes, W2g_words)
-        x_tiles[2] = load_x(2)
+        nc.vector.memset(bv_row[:], 0.0)
+        nc.vector.memset(ones[:], 1.0)
+        nc.sync.dma_start(out=bv_row[0:1, :], in_=bv.rearrange("(o f) -> o f", o=1))
         load_scales(wv_plane, Wv_scales)
         load_codes(wv_codes, Wv_words)
+        nc.vector.memset(b2g_rows[:], 0.0)
+        nc.sync.dma_start(out=b2g_rows[0:CHUNKS, :], in_=b2g.rearrange("(c m) -> c m", m=P))
+        x_tiles[2] = load_x(2)
+        load_scales(w2_plane, W2g_scales)
+        load_codes(w2_codes, W2g_words)
         for g in range(3, GROUPS):
             x_tiles[g] = load_x(g)
 
@@ -107,7 +110,7 @@ def tile_selectivemixing_pa_t_kernel(
         nc.vector.tensor_copy(out=b1_cols[:], in_=b1_bf16[:])
 
         grouped, codes_of, planes_of = {}, {}, {}
-        h_tiles, gates, products, out_tiles = {}, {}, {}, {}
+        h_tiles, tanhs, halves, out_tiles = {}, {}, {}, {}
 
         def transpose_x(copy, g, half):
             if half == 0:
@@ -136,15 +139,14 @@ def tile_selectivemixing_pa_t_kernel(
             codes_of[(kind, g)] = codes
             planes_of[(kind, g)] = plane
 
-        def mx_pass(weight_codes, weight_plane, chunk, kind, g):
-            cols = slice(P * chunk, P * (chunk + 1))
+        def mx_pass(lhs_codes, lhs_plane, rhs_codes, rhs_plane):
             bank = new_bank()
             nc.tensor.matmul_mx(
                 out=bank[:],
-                lhsT=weight_codes[:, cols].bitcast(FP8X4),
-                lhsT_scale=weight_plane[:, cols],
-                rhs=codes_of[(kind, g)][:].bitcast(FP8X4),
-                rhs_scale=planes_of[(kind, g)][:],
+                lhsT=lhs_codes.bitcast(FP8X4),
+                lhsT_scale=lhs_plane,
+                rhs=rhs_codes.bitcast(FP8X4),
+                rhs_scale=rhs_plane,
                 start=True,
                 stop=True,
             )
@@ -154,7 +156,10 @@ def tile_selectivemixing_pa_t_kernel(
             if t == 0:
                 h_rows = work.tile([P, PACK, GROUP], BF16, name="h_rows")
                 h_tiles[g] = h_rows
-            bank = mx_pass(w1_codes, w1_plane, t, "x", g)
+            cols = slice(P * t, P * (t + 1))
+            bank = mx_pass(
+                w1_codes[:, cols], w1_plane[:, cols], codes_of[("x", g)][:], planes_of[("x", g)][:]
+            )
             nc.scalar.activation(
                 out=h_tiles[g][:, t, :], in_=bank[:], func=ACT.Silu, bias=b1_cols[:, t : t + 1]
             )
@@ -162,38 +167,39 @@ def tile_selectivemixing_pa_t_kernel(
         def interleave_h(g):
             h_grouped = work.tile([P, PACK * GROUP], BF16, name="h_grouped", align_bytes=64)
             grouped[("h", g)] = h_grouped
-            nc.vector.tensor_copy(
-                out=h_grouped[:].rearrange("p (c t) -> p c t", t=PACK),
-                in_=h_tiles[g][:].rearrange("p t c -> p c t"),
-            )
+            dst = h_grouped[:].rearrange("p (c t) -> p c t", t=PACK)
+            src = h_tiles[g][:].rearrange("p t c -> p c t")
+            for j in range(TILES):
+                cols = slice(P * j, P * (j + 1))
+                nc.gpsimd.tensor_scalar(
+                    out=dst[:, cols, :], in0=src[:, cols, :], scalar1=1.0, scalar2=0.0, op0=ALU.mult, op1=ALU.add
+                )
 
         def gate(g, c):
             if c == 0:
-                gate_tile = work.tile([P, CHUNKS, GROUP], F32, name="gate_tile")
-                gates[g] = gate_tile
-            bank = mx_pass(w2_codes, w2_plane, c, "h", g)
+                tanh_tile = work.tile([P, CHUNKS, GROUP], F32, name="tanh_tile")
+                tanhs[g] = tanh_tile
+            cols = slice(P * c, P * (c + 1))
+            bank = mx_pass(
+                w2_codes[:, cols], w2_plane[:, cols], codes_of[("h", g)][:], planes_of[("h", g)][:]
+            )
             nc.scalar.activation(
-                out=gates[g][:, c, :], in_=bank[:], func=ACT.Tanh, bias=half_b2g[:, c : c + 1], scale=0.5
-            )
-            nc.gpsimd.tensor_scalar(
-                out=gates[g][:, c, :], in0=gates[g][:, c, :], scalar1=0.5, scalar2=0.5, op0=ALU.mult, op1=ALU.add
+                out=tanhs[g][:, c, :], in_=bank[:], func=ACT.Tanh, bias=half_b2g[:, c : c + 1], scale=0.5
             )
 
-        def values(g, c):
-            if c == 0:
-                product = work.tile([P, CHUNKS, GROUP], F32, name="product")
-                products[g] = product
-            bank = mx_pass(wv_codes, wv_plane, c, "x", g)
+        def values(g, j):
+            if j == 0:
+                half_values = held.tile([P, TILES, WIDTH], F32, name="half_values")
+                halves[g] = half_values
+            cols = slice(P * j, P * (j + 1))
+            bank = mx_pass(
+                codes_of[("x", g)][:, cols], planes_of[("x", g)][:, cols], wv_codes[:], wv_plane[:]
+            )
             nc.vector.scalar_tensor_tensor(
-                out=products[g][:, c, :],
-                in0=bank[:],
-                scalar=bv_cols[:, c : c + 1],
-                in1=gates[g][:, c, :],
-                op0=ALU.add,
-                op1=ALU.mult,
+                out=halves[g][:, j, :], in0=bank[:], scalar=0.5, in1=half_bv[:], op0=ALU.mult, op1=ALU.add
             )
 
-        def token_rows(copy, g, j):
+        def product(g, j):
             if j == 0:
                 out_sb = work.tile([P, TILES, WIDTH], F32, name="out_sb")
                 out_tiles[g] = out_sb
@@ -201,10 +207,12 @@ def tile_selectivemixing_pa_t_kernel(
             for c in range(CHUNKS):
                 nc.tensor.transpose(
                     out=bank[:, P * c : P * (c + 1)],
-                    in_=products[g][:, c, P * j : P * (j + 1)],
+                    in_=tanhs[g][:, c, P * j : P * (j + 1)],
                     identity=ident[:],
                 )
-            copy(out=out_tiles[g][:, j, :], in_=bank[:])
+            nc.vector.scalar_tensor_tensor(
+                out=out_tiles[g][:, j, :], in0=bank[:], scalar=1.0, in1=halves[g][:, j, :], op0=ALU.add, op1=ALU.mult
+            )
 
         def store(g, half):
             tiles = slice(2 * half, 2 * half + 2)
@@ -214,50 +222,40 @@ def tile_selectivemixing_pa_t_kernel(
             return 0 <= g < GROUPS
 
         def one_round(a):
-            load = {"scalar": 4 * live(a) + 4 * live(a - 2), "vector": 4 * live(a - 3) + 3 * live(a - 1) + live(a + 2)}
-
-            def copier():
-                if load["scalar"] <= load["vector"]:
-                    load["scalar"] += 1
-                    return nc.scalar.copy
-                load["vector"] += 1
-                return nc.vector.tensor_copy
-
+            if live(a + 1):
+                quantise("x", a + 1)
             if live(a - 1):
-                interleave_h(a - 1)
+                quantise("h", a - 1)
             if live(a):
                 for t in range(PACK):
                     first_layer(a, t)
+                interleave_h(a)
             if live(a + 2):
-                transpose_x(copier(), a + 2, 0)
-                transpose_x(copier(), a + 2, 1)
-            if live(a - 1):
-                quantise("h", a - 1)
+                transpose_x(nc.scalar.copy, a + 2, 0)
+                transpose_x(nc.scalar.copy, a + 2, 1)
             for i in range(4):
-                if live(a - 3):
-                    values(a - 3, i)
+                if live(a):
+                    values(a, i)
                 if live(a - 2):
                     gate(a - 2, i)
-                if i == 0 and live(a + 2):
-                    quantise("x", a + 2)
-            if live(a - 4):
-                token_rows(copier(), a - 4, 0)
-                token_rows(copier(), a - 4, 1)
-                store(a - 4, 0)
-                token_rows(copier(), a - 4, 2)
-                token_rows(copier(), a - 4, 3)
-                store(a - 4, 1)
+            if live(a - 3):
+                for j in range(TILES):
+                    product(a - 3, j)
+                    if j % 2 == 1:
+                        store(a - 3, j // 2)
 
         one_round(-2)
         one_round(-1)
-        bias_rows_f32 = keep.tile([P, P], F32, name="bias_rows_f32")
-        nc.vector.tensor_copy(out=bias_rows_f32[:], in_=bias_rows[:])
+        bv_bank = new_bank()
+        nc.tensor.matmul(out=bv_bank[:], lhsT=ones[:], rhs=bv_row[:], start=True, stop=True)
+        half_bv = keep.tile([P, WIDTH], F32, name="half_bv")
+        nc.vector.tensor_scalar_mul(out=half_bv[:], in0=bv_bank[:], scalar1=0.5)
+        b2g_rows_f32 = keep.tile([P, P], F32, name="b2g_rows_f32")
+        nc.vector.tensor_copy(out=b2g_rows_f32[:], in_=b2g_rows[:])
         one_round(0)
-        bias_bank = new_bank()
-        nc.tensor.transpose(out=bias_bank[:, 0:P], in_=bias_rows_f32[:], identity=ident[:])
+        b2g_bank = new_bank()
+        nc.tensor.transpose(out=b2g_bank[:, 0:P], in_=b2g_rows_f32[:], identity=ident[:])
         half_b2g = keep.tile([P, CHUNKS], F32, name="half_b2g")
-        nc.vector.tensor_scalar_mul(out=half_b2g[:], in0=bias_bank[:, 0:CHUNKS], scalar1=0.5)
-        bv_cols = keep.tile([P, CHUNKS], F32, name="bv_cols")
-        nc.vector.tensor_copy(out=bv_cols[:], in_=bias_bank[:, CHUNKS : 2 * CHUNKS])
-        for a in range(1, GROUPS + 4):
+        nc.vector.tensor_scalar_mul(out=half_b2g[:], in0=b2g_bank[:, 0:CHUNKS], scalar1=0.5)
+        for a in range(1, GROUPS + 3):
             one_round(a)

@@ -233,16 +233,19 @@ def tile_selectivemixing_pa_t_kernel(
             if live(a + 2):
                 transpose_x(nc.scalar.copy, a + 2, 0)
                 transpose_x(nc.scalar.copy, a + 2, 1)
-            for i in range(4):
-                if live(a):
-                    values(a, i)
-                if live(a - 2):
-                    gate(a - 2, i)
+            if live(a - 2) and not live(a):
+                for c in range(CHUNKS):
+                    gate(a - 2, c)
             if live(a - 3):
                 for j in range(TILES):
                     product(a - 3, j)
                     if j % 2 == 1:
                         store(a - 3, j // 2)
+            for i in range(4):
+                if live(a):
+                    values(a, i)
+                if live(a - 2) and live(a):
+                    gate(a - 2, i)
 
         one_round(-2)
         one_round(-1)

@@ -80,8 +80,8 @@ def tile_selectivemixing_pa_t_kernel(
         make_identity(nc, ident[:])
 
         x_tiles = {}
-        load_scales(w1_given_plane, W1_scales)
         x_tiles[0] = load_x(0)
+        load_scales(w1_given_plane, W1_scales)
         load_codes(w1_given_codes, W1_words)
         nc.sync.dma_start(out=b1_bf16[:], in_=b1.rearrange("(p t) -> p t", t=PACK))
         x_tiles[1] = load_x(1)
@@ -214,8 +214,8 @@ def tile_selectivemixing_pa_t_kernel(
                 out=out_tiles[g][:, j, :], in0=bank[:], scalar=1.0, in1=halves[g][:, j, :], op0=ALU.add, op1=ALU.mult
             )
 
-        def store(g, half):
-            tiles = slice(2 * half, 2 * half + 2)
+        def store(g, first, count):
+            tiles = slice(first, first + count)
             nc.sync.dma_start(out=out_groups[g][:, tiles, :], in_=out_tiles[g][:, tiles, :])
 
         def live(g):
@@ -239,8 +239,10 @@ def tile_selectivemixing_pa_t_kernel(
             if live(a - 3):
                 for j in range(TILES):
                     product(a - 3, j)
-                    if j % 2 == 1:
-                        store(a - 3, j // 2)
+                    if a - 3 == GROUPS - 1:
+                        store(a - 3, j, 1)
+                    elif j % 2 == 1:
+                        store(a - 3, j - 1, 2)
             for i in range(4):
                 if live(a):
                     values(a, i)

@@ -232,7 +232,7 @@ def tile_selectivemixing_pa_t_kernel(
                 interleave_h(a)
             if live(a + 2):
                 transpose_x(nc.scalar.copy, a + 2, 0)
-                transpose_x(nc.scalar.copy, a + 2, 1)
+                transpose_x(nc.vector.tensor_copy if a < 3 else nc.scalar.copy, a + 2, 1)
             if live(a - 2) and not live(a):
                 for c in range(CHUNKS):
                     gate(a - 2, c)

@@ -222,6 +222,18 @@ def tile_selectivemixing_pa_t_kernel(
             return 0 <= g < GROUPS
 
         def one_round(a):
+            load = {
+                "scalar": 4 * live(a) + 4 * live(a - 2),
+                "vector": 4 * live(a) + 4 * live(a - 3) + live(a + 1) + live(a - 1),
+            }
+
+            def copier():
+                if load["scalar"] < load["vector"]:
+                    load["scalar"] += 1
+                    return nc.scalar.copy
+                load["vector"] += 1
+                return nc.vector.tensor_copy
+
             if live(a + 1):
                 quantise("x", a + 1)
             if live(a - 1):
@@ -231,8 +243,8 @@ def tile_selectivemixing_pa_t_kernel(
                     first_layer(a, t)
                 interleave_h(a)
             if live(a + 2):
-                transpose_x(nc.scalar.copy, a + 2, 0)
-                transpose_x(nc.vector.tensor_copy if a < 3 else nc.scalar.copy, a + 2, 1)
+                transpose_x(copier(), a + 2, 0)
+                transpose_x(copier(), a + 2, 1)
             if live(a - 2) and not live(a):
                 for c in range(CHUNKS):
                     gate(a - 2, c)

@@ -98,17 +98,6 @@ def tile_selectivemixing_pa_t_kernel(
         for g in range(3, GROUPS):
             x_tiles[g] = load_x(g)
 
-        nc.vector.tensor_copy(
-            out=w1_plane[:].rearrange("p (t m) -> p m t", t=PACK),
-            in_=w1_given_plane[:].rearrange("p (m t) -> p m t", t=PACK),
-        )
-        nc.vector.tensor_copy(
-            out=w1_codes[:].bitcast(I32).rearrange("p (t m) -> p t m", t=PACK),
-            in_=w1_given_codes[:].bitcast(I32).rearrange("p (m t) -> p t m", t=PACK),
-        )
-        b1_cols = keep.tile([P, PACK], F32, name="b1_cols")
-        nc.vector.tensor_copy(out=b1_cols[:], in_=b1_bf16[:])
-
         grouped, codes_of, planes_of = {}, {}, {}
         h_tiles, tanhs, halves, out_tiles = {}, {}, {}, {}
 
@@ -251,10 +240,7 @@ def tile_selectivemixing_pa_t_kernel(
             if live(a - 3):
                 for j in range(TILES):
                     product(a - 3, j)
-                    if a - 3 == GROUPS - 1:
-                        store(a - 3, j, 1)
-                    elif j % 2 == 1:
-                        store(a - 3, j - 1, 2)
+                    store(a - 3, j, 1)
             for i in range(4):
                 if live(a):
                     values(a, i)
@@ -262,6 +248,16 @@ def tile_selectivemixing_pa_t_kernel(
                     gate(a - 2, i)
 
         one_round(-2)
+        nc.gpsimd.tensor_copy(
+            out=w1_plane[:].rearrange("p (t m) -> p m t", t=PACK),
+            in_=w1_given_plane[:].rearrange("p (m t) -> p m t", t=PACK),
+        )
+        nc.vector.tensor_copy(
+            out=w1_codes[:].bitcast(I32).rearrange("p (t m) -> p t m", t=PACK),
+            in_=w1_given_codes[:].bitcast(I32).rearrange("p (m t) -> p t m", t=PACK),
+        )
+        b1_cols = keep.tile([P, PACK], F32, name="b1_cols")
+        nc.vector.tensor_copy(out=b1_cols[:], in_=b1_bf16[:])
         one_round(-1)
         bv_bank = new_bank()
         nc.tensor.matmul(out=bv_bank[:], lhsT=ones[:], rhs=bv_row[:], start=True, stop=True)

@@ -82,17 +82,17 @@ def tile_selectivemixing_pa_t_kernel(
         x_tiles = {}
         x_tiles[0] = load_x(0)
         load_scales(w1_given_plane, W1_scales)
+        x_tiles[1] = load_x(1)
         load_codes(w1_given_codes, W1_words)
         nc.sync.dma_start(out=b1_bf16[:], in_=b1.rearrange("(p t) -> p t", t=PACK))
-        x_tiles[1] = load_x(1)
         nc.vector.memset(bv_row[:], 0.0)
         nc.vector.memset(ones[:], 1.0)
         nc.sync.dma_start(out=bv_row[0:1, :], in_=bv.rearrange("(o f) -> o f", o=1))
+        x_tiles[2] = load_x(2)
         load_scales(wv_plane, Wv_scales)
         load_codes(wv_codes, Wv_words)
         nc.vector.memset(b2g_rows[:], 0.0)
         nc.sync.dma_start(out=b2g_rows[0:CHUNKS, :], in_=b2g.rearrange("(c m) -> c m", m=P))
-        x_tiles[2] = load_x(2)
         load_scales(w2_plane, W2g_scales)
         load_codes(w2_codes, W2g_words)
         for g in range(3, GROUPS):
@@ -150,7 +150,7 @@ def tile_selectivemixing_pa_t_kernel(
                 w1_codes[:, cols], w1_plane[:, cols], codes_of[("x", g)][:], planes_of[("x", g)][:]
             )
             nc.scalar.activation(
-                out=h_tiles[g][:, t, :], in_=bank[:], func=ACT.Silu, bias=b1_cols[:, t : t + 1]
+                out=h_tiles[g][:, t, :], in_=bank[:], func=ACT.Silu, bias=b1_bf16[:, t : t + 1]
             )
 
         def interleave_h(g):
@@ -207,6 +207,13 @@ def tile_selectivemixing_pa_t_kernel(
             tiles = slice(first, first + count)
             nc.sync.dma_start(out=out_groups[g][:, tiles, :], in_=out_tiles[g][:, tiles, :])
 
+        def sort_w1_codes():
+            for t in range(PACK):
+                nc.vector.tensor_copy(
+                    out=w1_codes[:, P * t : P * (t + 1)].bitcast(I32),
+                    in_=w1_given_codes[:].bitcast(I32)[:, t:WIDTH:PACK],
+                )
+
         def live(g):
             return 0 <= g < GROUPS
 
@@ -225,7 +232,9 @@ def tile_selectivemixing_pa_t_kernel(
 
             if live(a + 1):
                 quantise("x", a + 1)
-            if live(a - 1):
+            if a == -1:
+                sort_w1_codes()
+            if live(a - 1) and a > 2:
                 quantise("h", a - 1)
             if live(a):
                 for t in range(PACK):
@@ -246,18 +255,13 @@ def tile_selectivemixing_pa_t_kernel(
                     values(a, i)
                 if live(a - 2) and live(a):
                     gate(a - 2, i)
+            if live(a - 1) and a <= 2:
+                quantise("h", a - 1)
 
         one_round(-2)
-        nc.gpsimd.tensor_copy(
-            out=w1_plane[:].rearrange("p (t m) -> p m t", t=PACK),
-            in_=w1_given_plane[:].rearrange("p (m t) -> p m t", t=PACK),
-        )
-        nc.vector.tensor_copy(
-            out=w1_codes[:].bitcast(I32).rearrange("p (t m) -> p t m", t=PACK),
-            in_=w1_given_codes[:].bitcast(I32).rearrange("p (m t) -> p t m", t=PACK),
-        )
-        b1_cols = keep.tile([P, PACK], F32, name="b1_cols")
-        nc.vector.tensor_copy(out=b1_cols[:], in_=b1_bf16[:])
+        for t in range(PACK):
+            cols = slice(P * t, P * (t + 1))
+            nc.vector.tensor_copy(out=w1_plane[:, cols], in_=w1_given_plane[:, t:WIDTH:PACK])
         one_round(-1)
         bv_bank = new_bank()
         nc.tensor.matmul(out=bv_bank[:], lhsT=ones[:], rhs=bv_row[:], start=True, stop=True)

@@ -154,7 +154,7 @@ def tile_selectivemixing_pa_t_kernel(
             )
 
         def interleave_h(g):
-            h_grouped = work.tile([P, PACK * GROUP], BF16, name="h_grouped", align_bytes=64)
+            h_grouped = work.tile([P, PACK * GROUP], BF16, name="h_grouped", align_bytes=64, bufs=1)
             grouped[("h", g)] = h_grouped
             dst = h_grouped[:].rearrange("p (c t) -> p c t", t=PACK)
             src = h_tiles[g][:].rearrange("p t c -> p c t")
@@ -230,12 +230,12 @@ def tile_selectivemixing_pa_t_kernel(
                 load["vector"] += 1
                 return nc.vector.tensor_copy
 
+            if live(a - 1) and a > 2:
+                quantise("h", a - 1)
             if live(a + 1):
                 quantise("x", a + 1)
             if a == -1:
                 sort_w1_codes()
-            if live(a - 1) and a > 2:
-                quantise("h", a - 1)
             if live(a):
                 for t in range(PACK):
                     first_layer(a, t)

@@ -80,11 +80,11 @@ def tile_selectivemixing_pa_t_kernel(
         make_identity(nc, ident[:])
 
         x_tiles = {}
+        nc.sync.dma_start(out=b1_bf16[:], in_=b1.rearrange("(p t) -> p t", t=PACK))
         x_tiles[0] = load_x(0)
         load_scales(w1_given_plane, W1_scales)
         x_tiles[1] = load_x(1)
         load_codes(w1_given_codes, W1_words)
-        nc.sync.dma_start(out=b1_bf16[:], in_=b1.rearrange("(p t) -> p t", t=PACK))
         nc.vector.memset(bv_row[:], 0.0)
         nc.vector.memset(ones[:], 1.0)
         nc.sync.dma_start(out=bv_row[0:1, :], in_=bv.rearrange("(o f) -> o f", o=1))
@@ -154,7 +154,10 @@ def tile_selectivemixing_pa_t_kernel(
             )
 
         def interleave_h(g):
-            h_grouped = work.tile([P, PACK * GROUP], BF16, name="h_grouped", align_bytes=64, bufs=1)
+            if g < 3:
+                h_grouped = work.tile([P, PACK * GROUP], BF16, name="h_grouped", align_bytes=64)
+            else:
+                h_grouped = keep.tile([P, PACK * GROUP], BF16, name="h_grouped_late", align_bytes=64)
             grouped[("h", g)] = h_grouped
             dst = h_grouped[:].rearrange("p (c t) -> p c t", t=PACK)
             src = h_tiles[g][:].rearrange("p t c -> p c t")
@@ -207,6 +210,20 @@ def tile_selectivemixing_pa_t_kernel(
             tiles = slice(first, first + count)
             nc.sync.dma_start(out=out_groups[g][:, tiles, :], in_=out_tiles[g][:, tiles, :])
 
+        half_bv = keep.tile([P, WIDTH], F32, name="half_bv")
+        b2g_rows_f32 = keep.tile([P, P], F32, name="b2g_rows_f32")
+        half_b2g = keep.tile([P, CHUNKS], F32, name="half_b2g")
+
+        def spread_bv():
+            bv_bank = new_bank()
+            nc.tensor.matmul(out=bv_bank[:], lhsT=ones[:], rhs=bv_row[:], start=True, stop=True)
+            nc.vector.tensor_scalar_mul(out=half_bv[:], in0=bv_bank[:], scalar1=0.5)
+
+        def spread_b2g():
+            b2g_bank = new_bank()
+            nc.tensor.transpose(out=b2g_bank[:, 0:P], in_=b2g_rows_f32[:], identity=ident[:])
+            nc.vector.tensor_scalar_mul(out=half_b2g[:], in0=b2g_bank[:, 0:CHUNKS], scalar1=0.5)
+
         def sort_w1_codes():
             for t in range(PACK):
                 nc.vector.tensor_copy(
@@ -240,9 +257,13 @@ def tile_selectivemixing_pa_t_kernel(
                 for t in range(PACK):
                     first_layer(a, t)
                 interleave_h(a)
+            if a == 0:
+                spread_bv()
             if live(a + 2):
                 transpose_x(copier(), a + 2, 0)
                 transpose_x(copier(), a + 2, 1)
+            if a == 1:
+                spread_b2g()
             if live(a - 2) and not live(a):
                 for c in range(CHUNKS):
                     gate(a - 2, c)
@@ -257,22 +278,14 @@ def tile_selectivemixing_pa_t_kernel(
                     gate(a - 2, i)
             if live(a - 1) and a <= 2:
                 quantise("h", a - 1)
+            if a == 0:
+                nc.vector.tensor_copy(out=b2g_rows_f32[:], in_=b2g_rows[:])
 
         one_round(-2)
         for t in range(PACK):
             cols = slice(P * t, P * (t + 1))
             nc.vector.tensor_copy(out=w1_plane[:, cols], in_=w1_given_plane[:, t:WIDTH:PACK])
         one_round(-1)
-        bv_bank = new_bank()
-        nc.tensor.matmul(out=bv_bank[:], lhsT=ones[:], rhs=bv_row[:], start=True, stop=True)
-        half_bv = keep.tile([P, WIDTH], F32, name="half_bv")
-        nc.vector.tensor_scalar_mul(out=half_bv[:], in0=bv_bank[:], scalar1=0.5)
-        b2g_rows_f32 = keep.tile([P, P], F32, name="b2g_rows_f32")
-        nc.vector.tensor_copy(out=b2g_rows_f32[:], in_=b2g_rows[:])
         one_round(0)
-        b2g_bank = new_bank()
-        nc.tensor.transpose(out=b2g_bank[:, 0:P], in_=b2g_rows_f32[:], identity=ident[:])
-        half_b2g = keep.tile([P, CHUNKS], F32, name="half_b2g")
-        nc.vector.tensor_scalar_mul(out=half_b2g[:], in0=b2g_bank[:, 0:CHUNKS], scalar1=0.5)
         for a in range(1, GROUPS + 3):
             one_round(a)

from contextlib import ExitStack

import concourse.mybir as mybir
from concourse.masks import make_identity

F32 = mybir.dt.float32
BF16 = mybir.dt.bfloat16
I32 = mybir.dt.int32
U32 = mybir.dt.uint32
U8 = mybir.dt.uint8
FP8X4 = mybir.dt.float8_e4m3fn_x4
ACT = mybir.ActivationFunctionType
ALU = mybir.AluOpType

P = 128
PACK = 4
WIDTH = 512
TOKENS = 4 * 1024
TILES = 4
GROUP = P * TILES
GROUPS = TOKENS // GROUP
CHUNKS = WIDTH // P
BANK = 512

FLOPS = 3 * 2 * TOKENS * WIDTH * WIDTH


def tile_selectivemixing_pa_t_kernel(
    tc, x, W1_words, W1_scales, b1, W2g_words, W2g_scales, b2g, Wv_words, Wv_scales, bv, out
):
    nc = tc.nc
    x_groups = x.flatten_outer_dims().rearrange("(g p j) k -> g p j k", p=P, j=TILES)
    out_groups = out.flatten_outer_dims().rearrange("(g p j) d -> g p j d", p=P, j=TILES)

    with ExitStack() as ctx:
        keep = ctx.enter_context(tc.tile_pool(name="keep", bufs=1))
        work = ctx.enter_context(tc.tile_pool(name="work", bufs=2))
        held = ctx.enter_context(tc.tile_pool(name="held", bufs=4))
        psum = ctx.enter_context(tc.psum_pool(name="psum", bufs=8))
        ctx.enter_context(tc.manual_schedule())

        def new_bank():
            bank = psum.tile([P, BANK], F32, name="bank", tag="bank")
            return bank

        def weight_tiles(name):
            codes = keep.tile([P, WIDTH], U32, name=name + "_codes", align_bytes=64)
            plane = keep.tile([P, WIDTH], U8, name=name + "_plane", align_bytes=64)
            return codes, plane

        def load_scales(plane, scales):
            nc.vector.memset(plane[:].bitcast(I32), 0)
            for r in range(4):
                nc.sync.dma_start(
                    out=plane[r:P:32, :].bitcast(I32), in_=scales[0, r:16:4, :].bitcast(I32)
                )

        def load_codes(codes, words):
            nc.sync.dma_start(
                out=codes[:].bitcast(I32),
                in_=words[0].rearrange("p n t -> p (n t)").bitcast(I32),
            )

        def load_x(g):
            x_sb = keep.tile([P, TILES, WIDTH], BF16, name="x%d" % g)
            for half in range(2):
                tiles = slice(2 * half, 2 * half + 2)
                nc.sync.dma_start(out=x_sb[:, tiles, :], in_=x_groups[g][:, tiles, :])
            return x_sb

        w1_given_codes, w1_given_plane = weight_tiles("w1_given")
        w1_codes, w1_plane = weight_tiles("w1")
        w2_codes, w2_plane = weight_tiles("w2")
        wv_codes, wv_plane = weight_tiles("wv")
        b1_bf16 = keep.tile([P, PACK], BF16, name="b1_bf16")
        b2g_rows = keep.tile([P, P], BF16, name="b2g_rows")
        bv_row = keep.tile([P, WIDTH], BF16, name="bv_row")
        ones = keep.tile([P, P], BF16, name="ones")
        ident = keep.tile([P, P], F32, name="ident")
        make_identity(nc, ident[:])

        x_tiles = {}
        nc.sync.dma_start(out=b1_bf16[:], in_=b1.rearrange("(p t) -> p t", t=PACK))
        x_tiles[0] = load_x(0)
        load_scales(w1_given_plane, W1_scales)
        x_tiles[1] = load_x(1)
        load_codes(w1_given_codes, W1_words)
        nc.vector.memset(bv_row[:], 0.0)
        nc.vector.memset(ones[:], 1.0)
        nc.sync.dma_start(out=bv_row[0:1, :], in_=bv.rearrange("(o f) -> o f", o=1))
        x_tiles[2] = load_x(2)
        load_scales(wv_plane, Wv_scales)
        load_codes(wv_codes, Wv_words)
        nc.vector.memset(b2g_rows[:], 0.0)
        nc.sync.dma_start(out=b2g_rows[0:CHUNKS, :], in_=b2g.rearrange("(c m) -> c m", m=P))
        load_scales(w2_plane, W2g_scales)
        load_codes(w2_codes, W2g_words)
        for g in range(3, GROUPS):
            x_tiles[g] = load_x(g)

        grouped, codes_of, planes_of = {}, {}, {}
        h_tiles, tanhs, halves, out_tiles = {}, {}, {}, {}

        def transpose_x(copy, g, half):
            if half == 0:
                x_grouped = work.tile([P, PACK * GROUP], BF16, name="x_grouped", align_bytes=64)
                grouped[("x", g)] = x_grouped
            given = x_tiles[g][:].bitcast(F32)
            bank = new_bank()
            pieces = bank[:].rearrange("p (j u w) -> p j u w", j=2, u=2)
            for j in range(2):
                for u in range(2):
                    nc.tensor.transpose(
                        out=pieces[:, j, u, :],
                        in_=given[:, 2 * half + j, u : WIDTH // 2 : 2],
                        identity=ident[:],
                    )
            words = grouped[("x", g)][:].bitcast(F32).rearrange("p (j w u) -> p j w u", j=TILES, u=2)
            copy(
                out=words[:, 2 * half : 2 * half + 2, :, :],
                in_=bank[:].rearrange("p (j u w) -> p j w u", j=2, u=2),
            )

        def quantise(kind, g):
            codes = keep.tile([P, GROUP], U32, name="%s_codes%d" % (kind, g), align_bytes=64)
            plane = keep.tile([P, GROUP], U8, name="%s_plane%d" % (kind, g), align_bytes=64)
            nc.vector.quantize_mx(out=codes[:].bitcast(FP8X4), scales=plane[:], in_=grouped[(kind, g)][:])
            codes_of[(kind, g)] = codes
            planes_of[(kind, g)] = plane

        def mx_pass(lhs_codes, lhs_plane, rhs_codes, rhs_plane):
            bank = new_bank()
            nc.tensor.matmul_mx(
                out=bank[:],
                lhsT=lhs_codes.bitcast(FP8X4),
                lhsT_scale=lhs_plane,
                rhs=rhs_codes.bitcast(FP8X4),
                rhs_scale=rhs_plane,
                start=True,
                stop=True,
            )
            return bank

        def first_layer(g, t):
            if t == 0:
                h_rows = work.tile([P, PACK, GROUP], BF16, name="h_rows")
                h_tiles[g] = h_rows
            cols = slice(P * t, P * (t + 1))
            bank = mx_pass(
                w1_codes[:, cols], w1_plane[:, cols], codes_of[("x", g)][:], planes_of[("x", g)][:]
            )
            nc.scalar.activation(
                out=h_tiles[g][:, t, :], in_=bank[:], func=ACT.Silu, bias=b1_bf16[:, t : t + 1]
            )

        def interleave_h(g):
            if g < 3:
                h_grouped = work.tile([P, PACK * GROUP], BF16, name="h_grouped", align_bytes=64)
            else:
                h_grouped = keep.tile([P, PACK * GROUP], BF16, name="h_grouped_late", align_bytes=64)
            grouped[("h", g)] = h_grouped
            dst = h_grouped[:].rearrange("p (c t) -> p c t", t=PACK)
            src = h_tiles[g][:].rearrange("p t c -> p c t")
            for j in range(TILES):
                cols = slice(P * j, P * (j + 1))
                nc.gpsimd.tensor_scalar(
                    out=dst[:, cols, :], in0=src[:, cols, :], scalar1=1.0, scalar2=0.0, op0=ALU.mult, op1=ALU.add
                )

        def gate(g, c):
            if c == 0:
                tanh_tile = work.tile([P, CHUNKS, GROUP], F32, name="tanh_tile")
                tanhs[g] = tanh_tile
            cols = slice(P * c, P * (c + 1))
            bank = mx_pass(
                w2_codes[:, cols], w2_plane[:, cols], codes_of[("h", g)][:], planes_of[("h", g)][:]
            )
            nc.scalar.activation(
                out=tanhs[g][:, c, :], in_=bank[:], func=ACT.Tanh, bias=half_b2g[:, c : c + 1], scale=0.5
            )

        def values(g, j):
            if j == 0:
                half_values = held.tile([P, TILES, WIDTH], F32, name="half_values")
                halves[g] = half_values
            cols = slice(P * j, P * (j + 1))
            bank = mx_pass(
                codes_of[("x", g)][:, cols], planes_of[("x", g)][:, cols], wv_codes[:], wv_plane[:]
            )
            nc.vector.scalar_tensor_tensor(
                out=halves[g][:, j, :], in0=bank[:], scalar=0.5, in1=half_bv[:], op0=ALU.mult, op1=ALU.add
            )

        def product(g, j):
            if j == 0:
                out_sb = work.tile([P, TILES, WIDTH], F32, name="out_sb")
                out_tiles[g] = out_sb
            bank = new_bank()
            for c in range(CHUNKS):
                nc.tensor.transpose(
                    out=bank[:, P * c : P * (c + 1)],
                    in_=tanhs[g][:, c, P * j : P * (j + 1)],
                    identity=ident[:],
                )
            nc.vector.scalar_tensor_tensor(
                out=out_tiles[g][:, j, :], in0=bank[:], scalar=1.0, in1=halves[g][:, j, :], op0=ALU.add, op1=ALU.mult
            )

        def store(g, first, count):
            tiles = slice(first, first + count)
            nc.sync.dma_start(out=out_groups[g][:, tiles, :], in_=out_tiles[g][:, tiles, :])

        half_bv = keep.tile([P, WIDTH], F32, name="half_bv")
        b2g_rows_f32 = keep.tile([P, P], F32, name="b2g_rows_f32")
        half_b2g = keep.tile([P, CHUNKS], F32, name="half_b2g")

        def spread_bv():
            bv_bank = new_bank()
            nc.tensor.matmul(out=bv_bank[:], lhsT=ones[:], rhs=bv_row[:], start=True, stop=True)
            nc.vector.tensor_scalar_mul(out=half_bv[:], in0=bv_bank[:], scalar1=0.5)

        def spread_b2g():
            b2g_bank = new_bank()
            nc.tensor.transpose(out=b2g_bank[:, 0:P], in_=b2g_rows_f32[:], identity=ident[:])
            nc.vector.tensor_scalar_mul(out=half_b2g[:], in0=b2g_bank[:, 0:CHUNKS], scalar1=0.5)

        def sort_w1_codes():
            for t in range(PACK):
                nc.vector.tensor_copy(
                    out=w1_codes[:, P * t : P * (t + 1)].bitcast(I32),
                    in_=w1_given_codes[:].bitcast(I32)[:, t:WIDTH:PACK],
                )

        def live(g):
            return 0 <= g < GROUPS

        def one_round(a):
            load = {
                "scalar": 4 * live(a) + 4 * live(a - 2),
                "vector": 4 * live(a) + 4 * live(a - 3) + live(a + 1) + live(a - 1),
            }

            def copier():
                if load["scalar"] < load["vector"]:
                    load["scalar"] += 1
                    return nc.scalar.copy
                load["vector"] += 1
                return nc.vector.tensor_copy

            if live(a - 1) and a > 2:
                quantise("h", a - 1)
            if live(a + 1):
                quantise("x", a + 1)
            if a == -1:
                sort_w1_codes()
            if live(a):
                for t in range(PACK):
                    first_layer(a, t)
                interleave_h(a)
            if a == 0:
                spread_bv()
            if live(a + 2):
                transpose_x(copier(), a + 2, 0)
                transpose_x(copier(), a + 2, 1)
            if a == 1:
                spread_b2g()
            if live(a - 2) and not live(a):
                for c in range(CHUNKS):
                    gate(a - 2, c)
            if live(a - 3):
                for j in range(TILES):
                    product(a - 3, j)
                    store(a - 3, j, 1)
            for i in range(4):
                if live(a):
                    values(a, i)
                if live(a - 2) and live(a):
                    gate(a - 2, i)
            if live(a - 1) and a <= 2:
                quantise("h", a - 1)
            if a == 0:
                nc.vector.tensor_copy(out=b2g_rows_f32[:], in_=b2g_rows[:])

        one_round(-2)
        for t in range(PACK):
            cols = slice(P * t, P * (t + 1))
            nc.vector.tensor_copy(out=w1_plane[:, cols], in_=w1_given_plane[:, t:WIDTH:PACK])
        one_round(-1)
        one_round(0)
        for a in range(1, GROUPS + 3):
            one_round(a)
